import numpy as np
import ml_dtypes


def mxq(x, axis, fmt="e4m3"):
    dtype, down = {"e4m3": (ml_dtypes.float8_e4m3fn, 7), "e5m2": (ml_dtypes.float8_e5m2, 14)}[fmt]
    v = np.moveaxis(np.asarray(x, np.float32).astype(ml_dtypes.bfloat16).astype(np.float64), axis, -1)
    blocks = v.reshape(v.shape[:-1] + (-1, 32))
    amax = np.abs(blocks).max(-1, keepdims=True)
    byte = np.maximum(np.where(amax > 0, np.frexp(amax)[1] - 1 + 127, 0) - down, 1)
    scale = np.exp2(byte - 127.0)
    codes = (blocks / scale).astype(np.float32).astype(dtype).astype(np.float64)
    return np.moveaxis((codes * scale).reshape(v.shape), -1, axis)


WIDE = False


def mx_kscale(k):
    if not WIDE:
        return np.ones(k)
    levels = np.array([20, -20, 10, -10, 0])
    a = np.random.permutation(np.resize(levels, k // 512 * 4)).reshape(k // 512, 4)
    idx = np.arange(k)
    return np.exp2(a[idx // 512, idx % 128 // 32])


BF16 = ml_dtypes.bfloat16


def bf(x):
    return np.asarray(x, np.float32).astype(BF16)


def f64(x):
    return np.asarray(x).astype(np.float64)


B, D, F, R, HT, S = 4, 512, 256, 128, 1, 256
T = B * HT * S


def silu(v):
    return v / (1.0 + np.exp(-v))


def setup_inputs():
    s = mx_kscale(T).reshape(B, 1, HT, S)
    mlp = silu(np.random.standard_normal((B, F, HT, S))) * np.random.standard_normal((B, F, HT, S))
    down_snapped = np.random.standard_normal((D, F)) * 1.5 / np.sqrt(F)
    down_scale_A = np.random.standard_normal((D, R))
    down_scale_B = np.random.standard_normal((R, F)) / np.sqrt(R)
    g = np.random.standard_normal((B, D, HT, S)) * np.exp2(np.random.randint(-12, 1, (B, 1, HT, S))) * 0.25
    return {
        "mlp": bf(mlp * s),
        "down_snapped": bf(down_snapped),
        "down_scale_A": bf(down_scale_A),
        "down_scale_B": bf(down_scale_B),
        "grad_out": bf(g / s),
    }


def reference(mlp, down_snapped, down_scale_A, down_scale_B, grad_out):
    g = f64(grad_out).reshape(B, D, HT * S).transpose(1, 0, 2).reshape(D, T)
    m = f64(mlp).reshape(B, F, HT * S).transpose(1, 0, 2).reshape(F, T)
    d_eff = mxq(g, 1, "e5m2") @ mxq(m, 1, "e4m3").T
    return d_eff * (f64(down_scale_A) @ f64(down_scale_B))

@@ -1,0 +1,155 @@
+import concourse.mybir as mybir
+from concourse.masks import make_identity
+
+BF16 = mybir.dt.bfloat16
+F32 = mybir.dt.float32
+I32 = mybir.dt.int32
+U32 = mybir.dt.uint32
+U8 = mybir.dt.uint8
+E4M3_X4 = mybir.dt.float8_e4m3fn_x4
+E5M2_X4 = mybir.dt.float8_e5m2_x4
+
+P = 128
+PACK = 4
+
+BATCH, D, F, R, WIDTH = 4, 512, 256, 128, 256
+PAIR = 2
+PASSES = BATCH // PAIR
+ROWS = 2
+UNIT = ROWS * P
+G_UNITS = D // UNIT
+D_TILES = D // P
+TILES_PER_UNIT = UNIT // P
+A_ROWS = D // P
+N_MOVING = 512
+WORK_BANKS = 4
+
+FLOPS = 2 * D * F * BATCH * WIDTH + 2 * D * F * R
+BYTES = 2 * (BATCH * F * WIDTH + BATCH * D * WIDTH + D * R + R * F) + 4 * D * F
+
+
+def load_unit(nc, sbuf, channels, name):
+    raw = sbuf.tile([P, PAIR * ROWS * WIDTH], BF16, name=name)
+    nc.sync.dma_start(out=raw[:].rearrange("p (u x) -> p u x", u=PAIR), in_=channels)
+    return raw
+
+
+def quantise_unit(nc, sbuf, work, identity, raw, codes, scales, name):
+    words = raw[:].bitcast(F32)
+    turned = work.tile([P, PAIR, ROWS, P], F32, tag="work", name="turned_" + name)
+    for u in range(PAIR):
+        for r in range(ROWS):
+            first = (u * ROWS + r) * P
+            nc.tensor.transpose(
+                out=turned[:, u, r, :], in_=words[:, first : first + P], identity=identity[:]
+            )
+    grouped = sbuf.tile([P, UNIT * PACK], BF16, name="grouped_" + name, align_bytes=64)
+    nc.scalar.copy(
+        out=grouped[:].bitcast(F32).rearrange("j (p r u) -> j p r u", r=ROWS, u=PAIR),
+        in_=turned[:].rearrange("j u r p -> j p r u"),
+    )
+    nc.vector.quantize_mx(out=codes, scales=scales, in_=grouped[:])
+
+
+def tile_ffnwithscales_pb_s_kernel(
+    tc, mlp, down_snapped, down_scale_A, down_scale_B, grad_out, out
+):
+    nc = tc.nc
+    with (
+        tc.tile_pool(name="sbuf", bufs=1) as sbuf,
+        tc.psum_pool(name="work", bufs=WORK_BANKS) as work,
+        tc.psum_pool(name="sums", bufs=1) as sums,
+    ):
+        identity_bf16 = sbuf.tile([P, P], BF16)
+        make_identity(nc, identity_bf16[:])
+        identity_f32 = sbuf.tile([P, P], F32)
+        make_identity(nc, identity_f32[:])
+
+        m_codes = [
+            sbuf.tile([P, N_MOVING], U32, name="m_codes%d" % c, align_bytes=64)
+            for c in range(PASSES)
+        ]
+        m_scales = [
+            sbuf.tile([P, N_MOVING], U8, name="m_scales%d" % c, align_bytes=64)
+            for c in range(PASSES)
+        ]
+        for c in range(PASSES):
+            nc.vector.memset(m_codes[c][:, F:N_MOVING].bitcast(I32), 0)
+            nc.vector.memset(m_scales[c][:, F:N_MOVING].bitcast(I32), 0)
+
+        a_raw = sbuf.tile([P, A_ROWS * R], BF16)
+        nc.sync.dma_start(
+            out=a_raw[:], in_=down_scale_A.rearrange("(p x) r -> p (x r)", x=A_ROWS)
+        )
+        b_sb = sbuf.tile([R, F], BF16)
+        nc.sync.dma_start(out=b_sb[:], in_=down_scale_B)
+
+        m_view = mlp.rearrange("b (p r) one w -> p b (r one w)", r=ROWS)
+        g_view = grad_out.rearrange("b (h p r) one w -> h p b (r one w)", p=P, r=ROWS)
+        m_raw = []
+        g_raw = []
+        for c in range(PASSES):
+            entries = slice(c * PAIR, (c + 1) * PAIR)
+            m_raw.append(load_unit(nc, sbuf, m_view[:, entries, :], "m_raw%d" % c))
+            g_raw.append(
+                [
+                    load_unit(nc, sbuf, g_view[h, :, entries, :], "g_raw%d_%d" % (c, h))
+                    for h in range(G_UNITS)
+                ]
+            )
+
+        a_turned = work.tile([R, A_ROWS, P], BF16, tag="work")
+        for x in range(A_ROWS):
+            nc.tensor.transpose(
+                out=a_turned[:, x, :], in_=a_raw[:, x * R : (x + 1) * R], identity=identity_bf16[:]
+            )
+        a_t = sbuf.tile([R, D], BF16)
+        nc.scalar.copy(
+            out=a_t[:].rearrange("r (p x) -> r p x", x=A_ROWS),
+            in_=a_turned[:].rearrange("r x p -> r p x"),
+        )
+        multipliers = sbuf.tile([P, D_TILES, F], F32)
+        tiles_per_bank = 512 // F
+        for first_tile in range(0, D_TILES, tiles_per_bank):
+            product = work.tile([P, tiles_per_bank, F], F32, tag="work")
+            for i in range(tiles_per_bank):
+                rows = slice((first_tile + i) * P, (first_tile + i + 1) * P)
+                nc.tensor.matmul(
+                    out=product[:, i, :], lhsT=a_t[:, rows], rhs=b_sb[:], start=True, stop=True
+                )
+            nc.scalar.copy(
+                out=multipliers[:, first_tile : first_tile + tiles_per_bank, :], in_=product[:]
+            )
+
+        d_eff = [sums.tile([P, N_MOVING], F32, name="d_eff%d" % t) for t in range(D_TILES)]
+        out_tiles = out.rearrange("(t q) f -> t q f", q=P)
+        for c in range(PASSES):
+            quantise_unit(
+                nc, sbuf, work, identity_f32, m_raw[c],
+                m_codes[c][:, 0:F].bitcast(E4M3_X4), m_scales[c][:, 0:F], "m%d" % c,
+            )
+            for h in range(G_UNITS):
+                g_codes = sbuf.tile([P, UNIT], U32, name="g_codes%d_%d" % (c, h), align_bytes=64)
+                g_scales = sbuf.tile([P, UNIT], U8, name="g_scales%d_%d" % (c, h), align_bytes=64)
+                quantise_unit(
+                    nc, sbuf, work, identity_f32, g_raw[c][h],
+                    g_codes[:].bitcast(E5M2_X4), g_scales[:], "g%d_%d" % (c, h),
+                )
+                for i in range(TILES_PER_UNIT):
+                    t = h * TILES_PER_UNIT + i
+                    cols = slice(i * P, (i + 1) * P)
+                    nc.tensor.matmul_mx(
+                        out=d_eff[t][:],
+                        lhsT=g_codes[:, cols].bitcast(E5M2_X4),
+                        lhsT_scale=g_scales[:, cols],
+                        rhs=m_codes[c][:].bitcast(E4M3_X4),
+                        rhs_scale=m_scales[c][:],
+                        start=(c == 0),
+                        stop=(c == PASSES - 1),
+                    )
+                    if c == PASSES - 1:
+                        result = sbuf.tile([P, F], F32, name="result%d" % t)
+                        nc.vector.tensor_mul(
+                            out=result[:], in0=d_eff[t][:, 0:F], in1=multipliers[:, t, :]
+                        )
+                        nc.sync.dma_start(out=out_tiles[t], in_=result[:])

@@ -59,6 +59,7 @@ def tile_ffnwithscales_pb_s_kernel(
         tc.tile_pool(name="sbuf", bufs=1) as sbuf,
         tc.psum_pool(name="work", bufs=WORK_BANKS) as work,
         tc.psum_pool(name="sums", bufs=1) as sums,
+        tc.manual_schedule(),
     ):
         identity_bf16 = sbuf.tile([P, P], BF16)
         make_identity(nc, identity_bf16[:])
@@ -117,39 +118,51 @@ def tile_ffnwithscales_pb_s_kernel(
                 nc.tensor.matmul(
                     out=product[:, i, :], lhsT=a_t[:, rows], rhs=b_sb[:], start=True, stop=True
                 )
-            nc.scalar.copy(
+            nc.vector.tensor_copy(
                 out=multipliers[:, first_tile : first_tile + tiles_per_bank, :], in_=product[:]
             )
 
-        d_eff = [sums.tile([P, N_MOVING], F32, name="d_eff%d" % t) for t in range(D_TILES)]
-        out_tiles = out.rearrange("(t q) f -> t q f", q=P)
+        g_codes = []
+        g_scales = []
         for c in range(PASSES):
             quantise_unit(
                 nc, sbuf, work, identity_f32, m_raw[c],
                 m_codes[c][:, 0:F].bitcast(E4M3_X4), m_scales[c][:, 0:F], "m%d" % c,
             )
+            g_codes.append(
+                [
+                    sbuf.tile([P, UNIT], U32, name="g_codes%d_%d" % (c, h), align_bytes=64)
+                    for h in range(G_UNITS)
+                ]
+            )
+            g_scales.append(
+                [
+                    sbuf.tile([P, UNIT], U8, name="g_scales%d_%d" % (c, h), align_bytes=64)
+                    for h in range(G_UNITS)
+                ]
+            )
             for h in range(G_UNITS):
-                g_codes = sbuf.tile([P, UNIT], U32, name="g_codes%d_%d" % (c, h), align_bytes=64)
-                g_scales = sbuf.tile([P, UNIT], U8, name="g_scales%d_%d" % (c, h), align_bytes=64)
                 quantise_unit(
                     nc, sbuf, work, identity_f32, g_raw[c][h],
-                    g_codes[:].bitcast(E5M2_X4), g_scales[:], "g%d_%d" % (c, h),
+                    g_codes[c][h][:].bitcast(E5M2_X4), g_scales[c][h][:], "g%d_%d" % (c, h),
                 )
-                for i in range(TILES_PER_UNIT):
-                    t = h * TILES_PER_UNIT + i
-                    cols = slice(i * P, (i + 1) * P)
-                    nc.tensor.matmul_mx(
-                        out=d_eff[t][:],
-                        lhsT=g_codes[:, cols].bitcast(E5M2_X4),
-                        lhsT_scale=g_scales[:, cols],
-                        rhs=m_codes[c][:].bitcast(E4M3_X4),
-                        rhs_scale=m_scales[c][:],
-                        start=(c == 0),
-                        stop=(c == PASSES - 1),
-                    )
-                    if c == PASSES - 1:
-                        result = sbuf.tile([P, F], F32, name="result%d" % t)
-                        nc.vector.tensor_mul(
-                            out=result[:], in0=d_eff[t][:, 0:F], in1=multipliers[:, t, :]
-                        )
-                        nc.sync.dma_start(out=out_tiles[t], in_=result[:])
+
+        d_eff = [sums.tile([P, N_MOVING], F32, name="d_eff%d" % t) for t in range(D_TILES)]
+        out_tiles = out.rearrange("(t q) f -> t q f", q=P)
+        for c in range(PASSES):
+            for t in range(D_TILES):
+                h, i = divmod(t, TILES_PER_UNIT)
+                cols = slice(i * P, (i + 1) * P)
+                nc.tensor.matmul_mx(
+                    out=d_eff[t][:],
+                    lhsT=g_codes[c][h][:, cols].bitcast(E5M2_X4),
+                    lhsT_scale=g_scales[c][h][:, cols],
+                    rhs=m_codes[c][:].bitcast(E4M3_X4),
+                    rhs_scale=m_scales[c][:],
+                    start=(c == 0),
+                    stop=(c == PASSES - 1),
+                )
+        for t in range(D_TILES):
+            result = sbuf.tile([P, F], F32, name="result%d" % t)
+            nc.vector.tensor_mul(out=result[:], in0=d_eff[t][:, 0:F], in1=multipliers[:, t, :])
+            nc.sync.dma_start(out=out_tiles[t], in_=result[:])

@@ -19,10 +19,10 @@ ROWS = 2
 UNIT = ROWS * P
 G_UNITS = D // UNIT
 D_TILES = D // P
-TILES_PER_UNIT = UNIT // P
-A_ROWS = D // P
 N_MOVING = 512
+BANK = 512
 WORK_BANKS = 4
+LAG = 1
 
 FLOPS = 2 * D * F * BATCH * WIDTH + 2 * D * F * R
 BYTES = 2 * (BATCH * F * WIDTH + BATCH * D * WIDTH + D * R + R * F) + 4 * D * F
@@ -34,21 +34,27 @@ def load_unit(nc, sbuf, channels, name):
     return raw
 
 
-def quantise_unit(nc, sbuf, work, identity, raw, codes, scales, name):
-    words = raw[:].bitcast(F32)
-    turned = work.tile([P, PAIR, ROWS, P], F32, tag="work", name="turned_" + name)
-    for u in range(PAIR):
-        for r in range(ROWS):
-            first = (u * ROWS + r) * P
-            nc.tensor.transpose(
-                out=turned[:, u, r, :], in_=words[:, first : first + P], identity=identity[:]
-            )
-    grouped = sbuf.tile([P, UNIT * PACK], BF16, name="grouped_" + name, align_bytes=64)
-    nc.scalar.copy(
-        out=grouped[:].bitcast(F32).rearrange("j (p r u) -> j p r u", r=ROWS, u=PAIR),
-        in_=turned[:].rearrange("j u r p -> j p r u"),
-    )
-    nc.vector.quantize_mx(out=codes, scales=scales, in_=grouped[:])
+def quantise_unit(nc, sbuf, work, identity, raw, on_vector, codes, scales, fp8_x4, name):
+    words = raw[:].bitcast(F32).rearrange("p (u r j) -> p u r j", u=PAIR, r=ROWS)
+    grouped = [
+        sbuf.tile([P, P * PACK], BF16, name="grouped_%s_%d" % (name, r), align_bytes=64)
+        for r in range(ROWS)
+    ]
+    for r in range(ROWS):
+        turned = work.tile([P, PAIR, P], F32, tag="work", name="turned_%s_%d" % (name, r))
+        for u in range(PAIR):
+            nc.tensor.transpose(out=turned[:, u, :], in_=words[:, u, r, :], identity=identity[:])
+        grouped_words = grouped[r][:].bitcast(F32).rearrange("j (p u) -> j p u", u=PAIR)
+        turned_words = turned[:].rearrange("j u p -> j p u")
+        if on_vector:
+            nc.vector.tensor_copy(out=grouped_words, in_=turned_words)
+        else:
+            nc.scalar.copy(out=grouped_words, in_=turned_words)
+    for r in range(ROWS):
+        cols = slice(r * P, (r + 1) * P)
+        nc.vector.quantize_mx(
+            out=codes[:, cols].bitcast(fp8_x4), scales=scales[:, cols], in_=grouped[r][:]
+        )
 
 
 def tile_ffnwithscales_pb_s_kernel(
@@ -78,91 +84,86 @@ def tile_ffnwithscales_pb_s_kernel(
             nc.vector.memset(m_codes[c][:, F:N_MOVING].bitcast(I32), 0)
             nc.vector.memset(m_scales[c][:, F:N_MOVING].bitcast(I32), 0)
 
-        a_raw = sbuf.tile([P, A_ROWS * R], BF16)
+        a_raw = sbuf.tile([P, D_TILES * R], BF16)
         nc.sync.dma_start(
-            out=a_raw[:], in_=down_scale_A.rearrange("(p x) r -> p (x r)", x=A_ROWS)
+            out=a_raw[:].rearrange("q (h x) -> q h x", h=G_UNITS),
+            in_=down_scale_A.rearrange("(h q r) k -> q h (r k)", q=P, r=ROWS),
         )
         b_sb = sbuf.tile([R, F], BF16)
         nc.sync.dma_start(out=b_sb[:], in_=down_scale_B)
 
         m_view = mlp.rearrange("b (p r) one w -> p b (r one w)", r=ROWS)
         g_view = grad_out.rearrange("b (h p r) one w -> h p b (r one w)", p=P, r=ROWS)
-        m_raw = []
-        g_raw = []
-        for c in range(PASSES):
-            entries = slice(c * PAIR, (c + 1) * PAIR)
-            m_raw.append(load_unit(nc, sbuf, m_view[:, entries, :], "m_raw%d" % c))
-            g_raw.append(
-                [
-                    load_unit(nc, sbuf, g_view[h, :, entries, :], "g_raw%d_%d" % (c, h))
-                    for h in range(G_UNITS)
-                ]
-            )
+        entries = [slice(c * PAIR, (c + 1) * PAIR) for c in range(PASSES)]
+        g_order = [(h, c) for h in range(G_UNITS) for c in range(PASSES)]
+        m_raw = [
+            load_unit(nc, sbuf, m_view[:, entries[c], :], "m_raw%d" % c) for c in range(PASSES)
+        ]
+        g_raw = [
+            load_unit(nc, sbuf, g_view[h, :, entries[c], :], "g_raw%d_%d" % (h, c))
+            for h, c in g_order
+        ]
 
-        a_turned = work.tile([R, A_ROWS, P], BF16, tag="work")
-        for x in range(A_ROWS):
+        a_turned = work.tile([R, D_TILES, P], BF16, tag="work")
+        for t in range(D_TILES):
             nc.tensor.transpose(
-                out=a_turned[:, x, :], in_=a_raw[:, x * R : (x + 1) * R], identity=identity_bf16[:]
+                out=a_turned[:, t, :], in_=a_raw[:, t * R : (t + 1) * R], identity=identity_bf16[:]
             )
-        a_t = sbuf.tile([R, D], BF16)
-        nc.scalar.copy(
-            out=a_t[:].rearrange("r (p x) -> r p x", x=A_ROWS),
-            in_=a_turned[:].rearrange("r x p -> r p x"),
-        )
+        a_t = sbuf.tile([R, D_TILES, P], BF16)
+        nc.scalar.copy(out=a_t[:], in_=a_turned[:])
         multipliers = sbuf.tile([P, D_TILES, F], F32)
-        tiles_per_bank = 512 // F
+        tiles_per_bank = BANK // F
         for first_tile in range(0, D_TILES, tiles_per_bank):
             product = work.tile([P, tiles_per_bank, F], F32, tag="work")
             for i in range(tiles_per_bank):
-                rows = slice((first_tile + i) * P, (first_tile + i + 1) * P)
                 nc.tensor.matmul(
-                    out=product[:, i, :], lhsT=a_t[:, rows], rhs=b_sb[:], start=True, stop=True
+                    out=product[:, i, :], lhsT=a_t[:, first_tile + i, :], rhs=b_sb[:],
+                    start=True, stop=True,
                 )
-            nc.vector.tensor_copy(
+            nc.scalar.copy(
                 out=multipliers[:, first_tile : first_tile + tiles_per_bank, :], in_=product[:]
             )
 
-        g_codes = []
-        g_scales = []
+        d_eff = [sums.tile([P, N_MOVING], F32, name="d_eff%d" % t) for t in range(D_TILES)]
+        out_view = out.rearrange("(h q r) f -> h r q f", q=P, r=ROWS)
         for c in range(PASSES):
             quantise_unit(
-                nc, sbuf, work, identity_f32, m_raw[c],
-                m_codes[c][:, 0:F].bitcast(E4M3_X4), m_scales[c][:, 0:F], "m%d" % c,
+                nc, sbuf, work, identity_f32, m_raw[c], True,
+                m_codes[c], m_scales[c], E4M3_X4, "m%d" % c,
             )
-            g_codes.append(
-                [
-                    sbuf.tile([P, UNIT], U32, name="g_codes%d_%d" % (c, h), align_bytes=64)
-                    for h in range(G_UNITS)
-                ]
-            )
-            g_scales.append(
-                [
-                    sbuf.tile([P, UNIT], U8, name="g_scales%d_%d" % (c, h), align_bytes=64)
-                    for h in range(G_UNITS)
-                ]
-            )
-            for h in range(G_UNITS):
+        g_codes = [
+            sbuf.tile([P, UNIT], U32, name="g_codes%d_%d" % (h, c), align_bytes=64)
+            for h, c in g_order
+        ]
+        g_scales = [
+            sbuf.tile([P, UNIT], U8, name="g_scales%d_%d" % (h, c), align_bytes=64)
+            for h, c in g_order
+        ]
+        for n in range(len(g_order) + LAG):
+            if n < len(g_order):
                 quantise_unit(
-                    nc, sbuf, work, identity_f32, g_raw[c][h],
-                    g_codes[c][h][:].bitcast(E5M2_X4), g_scales[c][h][:], "g%d_%d" % (c, h),
+                    nc, sbuf, work, identity_f32, g_raw[n], False,
+                    g_codes[n], g_scales[n], E5M2_X4, "g%d_%d" % g_order[n],
                 )
-
-        d_eff = [sums.tile([P, N_MOVING], F32, name="d_eff%d" % t) for t in range(D_TILES)]
-        out_tiles = out.rearrange("(t q) f -> t q f", q=P)
-        for c in range(PASSES):
-            for t in range(D_TILES):
-                h, i = divmod(t, TILES_PER_UNIT)
-                cols = slice(i * P, (i + 1) * P)
-                nc.tensor.matmul_mx(
-                    out=d_eff[t][:],
-                    lhsT=g_codes[c][h][:, cols].bitcast(E5M2_X4),
-                    lhsT_scale=g_scales[c][h][:, cols],
-                    rhs=m_codes[c][:].bitcast(E4M3_X4),
-                    rhs_scale=m_scales[c][:],
-                    start=(c == 0),
-                    stop=(c == PASSES - 1),
-                )
-        for t in range(D_TILES):
-            result = sbuf.tile([P, F], F32, name="result%d" % t)
-            nc.vector.tensor_mul(out=result[:], in0=d_eff[t][:, 0:F], in1=multipliers[:, t, :])
-            nc.sync.dma_start(out=out_tiles[t], in_=result[:])
+            if n >= LAG:
+                h, c = g_order[n - LAG]
+                for r in range(ROWS):
+                    t = h * ROWS + r
+                    cols = slice(r * P, (r + 1) * P)
+                    nc.tensor.matmul_mx(
+                        out=d_eff[t][:],
+                        lhsT=g_codes[n - LAG][:, cols].bitcast(E5M2_X4),
+                        lhsT_scale=g_scales[n - LAG][:, cols],
+                        rhs=m_codes[c][:].bitcast(E4M3_X4),
+                        rhs_scale=m_scales[c][:],
+                        start=(c == 0),
+                        stop=(c == PASSES - 1),
+                    )
+                    if c == PASSES - 1:
+                        result = sbuf.tile([P, F], F32, name="result%d" % t)
+                        nc.vector.tensor_mul(
+                            out=result[:].rearrange("q (p s) -> q p s", s=ROWS),
+                            in0=d_eff[t][:, 0:F].rearrange("q (s p) -> q p s", s=ROWS),
+                            in1=multipliers[:, t, :].rearrange("q (p s) -> q p s", s=ROWS),
+                        )
+                        nc.sync.dma_start(out=out_view[h, r], in_=result[:])

@@ -19,10 +19,10 @@ ROWS = 2
 UNIT = ROWS * P
 G_UNITS = D // UNIT
 D_TILES = D // P
+TILES_PER_UNIT = UNIT // P
+A_ROWS = D // P
 N_MOVING = 512
-BANK = 512
 WORK_BANKS = 4
-LAG = 1
 
 FLOPS = 2 * D * F * BATCH * WIDTH + 2 * D * F * R
 BYTES = 2 * (BATCH * F * WIDTH + BATCH * D * WIDTH + D * R + R * F) + 4 * D * F
@@ -34,27 +34,21 @@ def load_unit(nc, sbuf, channels, name):
     return raw
 
 
-def quantise_unit(nc, sbuf, work, identity, raw, on_vector, codes, scales, fp8_x4, name):
-    words = raw[:].bitcast(F32).rearrange("p (u r j) -> p u r j", u=PAIR, r=ROWS)
-    grouped = [
-        sbuf.tile([P, P * PACK], BF16, name="grouped_%s_%d" % (name, r), align_bytes=64)
-        for r in range(ROWS)
-    ]
-    for r in range(ROWS):
-        turned = work.tile([P, PAIR, P], F32, tag="work", name="turned_%s_%d" % (name, r))
-        for u in range(PAIR):
-            nc.tensor.transpose(out=turned[:, u, :], in_=words[:, u, r, :], identity=identity[:])
-        grouped_words = grouped[r][:].bitcast(F32).rearrange("j (p u) -> j p u", u=PAIR)
-        turned_words = turned[:].rearrange("j u p -> j p u")
-        if on_vector:
-            nc.vector.tensor_copy(out=grouped_words, in_=turned_words)
-        else:
-            nc.scalar.copy(out=grouped_words, in_=turned_words)
-    for r in range(ROWS):
-        cols = slice(r * P, (r + 1) * P)
-        nc.vector.quantize_mx(
-            out=codes[:, cols].bitcast(fp8_x4), scales=scales[:, cols], in_=grouped[r][:]
-        )
+def quantise_unit(nc, sbuf, work, identity, raw, codes, scales, name):
+    words = raw[:].bitcast(F32)
+    turned = work.tile([P, PAIR, ROWS, P], F32, tag="work", name="turned_" + name)
+    for u in range(PAIR):
+        for r in range(ROWS):
+            first = (u * ROWS + r) * P
+            nc.tensor.transpose(
+                out=turned[:, u, r, :], in_=words[:, first : first + P], identity=identity[:]
+            )
+    grouped = sbuf.tile([P, UNIT * PACK], BF16, name="grouped_" + name, align_bytes=64)
+    nc.scalar.copy(
+        out=grouped[:].bitcast(F32).rearrange("j (p r u) -> j p r u", r=ROWS, u=PAIR),
+        in_=turned[:].rearrange("j u r p -> j p r u"),
+    )
+    nc.vector.quantize_mx(out=codes, scales=scales, in_=grouped[:])
 
 
 def tile_ffnwithscales_pb_s_kernel(
@@ -84,86 +78,101 @@ def tile_ffnwithscales_pb_s_kernel(
             nc.vector.memset(m_codes[c][:, F:N_MOVING].bitcast(I32), 0)
             nc.vector.memset(m_scales[c][:, F:N_MOVING].bitcast(I32), 0)
 
-        a_raw = sbuf.tile([P, D_TILES * R], BF16)
+        m_view = mlp.rearrange("b (p r) one w -> p b (r one w)", r=ROWS)
+        g_view = grad_out.rearrange("b (h p r) one w -> h p b (r one w)", p=P, r=ROWS)
+        a_raw = sbuf.tile([P, A_ROWS * R], BF16)
         nc.sync.dma_start(
-            out=a_raw[:].rearrange("q (h x) -> q h x", h=G_UNITS),
-            in_=down_scale_A.rearrange("(h q r) k -> q h (r k)", q=P, r=ROWS),
+            out=a_raw[:], in_=down_scale_A.rearrange("(p x) r -> p (x r)", x=A_ROWS)
         )
         b_sb = sbuf.tile([R, F], BF16)
         nc.sync.dma_start(out=b_sb[:], in_=down_scale_B)
-
-        m_view = mlp.rearrange("b (p r) one w -> p b (r one w)", r=ROWS)
-        g_view = grad_out.rearrange("b (h p r) one w -> h p b (r one w)", p=P, r=ROWS)
-        entries = [slice(c * PAIR, (c + 1) * PAIR) for c in range(PASSES)]
-        g_order = [(h, c) for h in range(G_UNITS) for c in range(PASSES)]
-        m_raw = [
-            load_unit(nc, sbuf, m_view[:, entries[c], :], "m_raw%d" % c) for c in range(PASSES)
-        ]
-        g_raw = [
-            load_unit(nc, sbuf, g_view[h, :, entries[c], :], "g_raw%d_%d" % (h, c))
-            for h, c in g_order
-        ]
-
-        a_turned = work.tile([R, D_TILES, P], BF16, tag="work")
-        for t in range(D_TILES):
-            nc.tensor.transpose(
-                out=a_turned[:, t, :], in_=a_raw[:, t * R : (t + 1) * R], identity=identity_bf16[:]
+        m_raw = []
+        g_raw = []
+        for c in range(PASSES):
+            entries = slice(c * PAIR, (c + 1) * PAIR)
+            m_raw.append(load_unit(nc, sbuf, m_view[:, entries, :], "m_raw%d" % c))
+            g_raw.append(
+                [
+                    load_unit(nc, sbuf, g_view[h, :, entries, :], "g_raw%d_%d" % (c, h))
+                    for h in range(G_UNITS)
+                ]
             )
-        a_t = sbuf.tile([R, D_TILES, P], BF16)
-        nc.scalar.copy(out=a_t[:], in_=a_turned[:])
+
+        g_codes = [
+            [
+                sbuf.tile([P, UNIT], U32, name="g_codes%d_%d" % (c, h), align_bytes=64)
+                for h in range(G_UNITS)
+            ]
+            for c in range(PASSES)
+        ]
+        g_scales = [
+            [
+                sbuf.tile([P, UNIT], U8, name="g_scales%d_%d" % (c, h), align_bytes=64)
+                for h in range(G_UNITS)
+            ]
+            for c in range(PASSES)
+        ]
+
+        def quantise_mlp(c):
+            quantise_unit(
+                nc, sbuf, work, identity_f32, m_raw[c],
+                m_codes[c][:, 0:F].bitcast(E4M3_X4), m_scales[c][:, 0:F], "m%d" % c,
+            )
+
+        def quantise_grad_out(c):
+            for h in range(G_UNITS):
+                quantise_unit(
+                    nc, sbuf, work, identity_f32, g_raw[c][h],
+                    g_codes[c][h][:].bitcast(E5M2_X4), g_scales[c][h][:], "g%d_%d" % (c, h),
+                )
+
+        a_turned = work.tile([R, A_ROWS, P], BF16, tag="work")
+        for x in range(A_ROWS):
+            nc.tensor.transpose(
+                out=a_turned[:, x, :], in_=a_raw[:, x * R : (x + 1) * R], identity=identity_bf16[:]
+            )
+        a_t = sbuf.tile([R, D], BF16)
+        nc.scalar.copy(
+            out=a_t[:].rearrange("r (p x) -> r p x", x=A_ROWS),
+            in_=a_turned[:].rearrange("r x p -> r p x"),
+        )
+
+        quantise_mlp(0)
+
         multipliers = sbuf.tile([P, D_TILES, F], F32)
-        tiles_per_bank = BANK // F
+        tiles_per_bank = 512 // F
         for first_tile in range(0, D_TILES, tiles_per_bank):
             product = work.tile([P, tiles_per_bank, F], F32, tag="work")
             for i in range(tiles_per_bank):
+                rows = slice((first_tile + i) * P, (first_tile + i + 1) * P)
                 nc.tensor.matmul(
-                    out=product[:, i, :], lhsT=a_t[:, first_tile + i, :], rhs=b_sb[:],
-                    start=True, stop=True,
+                    out=product[:, i, :], lhsT=a_t[:, rows], rhs=b_sb[:], start=True, stop=True
                 )
-            nc.scalar.copy(
+            nc.vector.tensor_copy(
                 out=multipliers[:, first_tile : first_tile + tiles_per_bank, :], in_=product[:]
             )
 
+        quantise_grad_out(0)
+        for c in range(1, PASSES):
+            quantise_mlp(c)
+            quantise_grad_out(c)
+
         d_eff = [sums.tile([P, N_MOVING], F32, name="d_eff%d" % t) for t in range(D_TILES)]
-        out_view = out.rearrange("(h q r) f -> h r q f", q=P, r=ROWS)
+        out_tiles = out.rearrange("(t q) f -> t q f", q=P)
         for c in range(PASSES):
-            quantise_unit(
-                nc, sbuf, work, identity_f32, m_raw[c], True,
-                m_codes[c], m_scales[c], E4M3_X4, "m%d" % c,
-            )
-        g_codes = [
-            sbuf.tile([P, UNIT], U32, name="g_codes%d_%d" % (h, c), align_bytes=64)
-            for h, c in g_order
-        ]
-        g_scales = [
-            sbuf.tile([P, UNIT], U8, name="g_scales%d_%d" % (h, c), align_bytes=64)
-            for h, c in g_order
-        ]
-        for n in range(len(g_order) + LAG):
-            if n < len(g_order):
-                quantise_unit(
-                    nc, sbuf, work, identity_f32, g_raw[n], False,
-                    g_codes[n], g_scales[n], E5M2_X4, "g%d_%d" % g_order[n],
+            for t in range(D_TILES):
+                h, i = divmod(t, TILES_PER_UNIT)
+                cols = slice(i * P, (i + 1) * P)
+                nc.tensor.matmul_mx(
+                    out=d_eff[t][:],
+                    lhsT=g_codes[c][h][:, cols].bitcast(E5M2_X4),
+                    lhsT_scale=g_scales[c][h][:, cols],
+                    rhs=m_codes[c][:].bitcast(E4M3_X4),
+                    rhs_scale=m_scales[c][:],
+                    start=(c == 0),
+                    stop=(c == PASSES - 1),
                 )
-            if n >= LAG:
-                h, c = g_order[n - LAG]
-                for r in range(ROWS):
-                    t = h * ROWS + r
-                    cols = slice(r * P, (r + 1) * P)
-                    nc.tensor.matmul_mx(
-                        out=d_eff[t][:],
-                        lhsT=g_codes[n - LAG][:, cols].bitcast(E5M2_X4),
-                        lhsT_scale=g_scales[n - LAG][:, cols],
-                        rhs=m_codes[c][:].bitcast(E4M3_X4),
-                        rhs_scale=m_scales[c][:],
-                        start=(c == 0),
-                        stop=(c == PASSES - 1),
-                    )
-                    if c == PASSES - 1:
-                        result = sbuf.tile([P, F], F32, name="result%d" % t)
-                        nc.vector.tensor_mul(
-                            out=result[:].rearrange("q (p s) -> q p s", s=ROWS),
-                            in0=d_eff[t][:, 0:F].rearrange("q (s p) -> q p s", s=ROWS),
-                            in1=multipliers[:, t, :].rearrange("q (p s) -> q p s", s=ROWS),
-                        )
-                        nc.sync.dma_start(out=out_view[h, r], in_=result[:])
+        for t in range(D_TILES):
+            result = sbuf.tile([P, F], F32, name="result%d" % t)
+            nc.vector.tensor_mul(out=result[:], in0=d_eff[t][:, 0:F], in1=multipliers[:, t, :])
+            nc.sync.dma_start(out=out_tiles[t], in_=result[:])

@@ -22,6 +22,7 @@ D_TILES = D // P
 TILES_PER_UNIT = UNIT // P
 A_ROWS = D // P
 N_MOVING = 512
+WARM_MATMULS = 4
 WORK_BANKS = 4
 
 FLOPS = 2 * D * F * BATCH * WIDTH + 2 * D * F * R
@@ -61,6 +62,14 @@ def tile_ffnwithscales_pb_s_kernel(
         tc.psum_pool(name="sums", bufs=1) as sums,
         tc.manual_schedule(),
     ):
+        warm = sbuf.tile([P, P], F32)
+        nc.gpsimd.memset(warm[:], 0.0)
+        warm_out = work.tile([P, WARM_MATMULS, P], F32, tag="work")
+        for i in range(WARM_MATMULS):
+            nc.tensor.matmul(
+                out=warm_out[:, i, :], lhsT=warm[:], rhs=warm[:], start=True, stop=True
+            )
+
         identity_bf16 = sbuf.tile([P, P], BF16)
         make_identity(nc, identity_bf16[:])
         identity_f32 = sbuf.tile([P, P], F32)

@@ -128,13 +128,6 @@ def tile_ffnwithscales_pb_s_kernel(
                 m_codes[c][:, 0:F].bitcast(E4M3_X4), m_scales[c][:, 0:F], "m%d" % c,
             )
 
-        def quantise_grad_out(c):
-            for h in range(G_UNITS):
-                quantise_unit(
-                    nc, sbuf, work, identity_f32, g_raw[c][h],
-                    g_codes[c][h][:].bitcast(E5M2_X4), g_scales[c][h][:], "g%d_%d" % (c, h),
-                )
-
         a_turned = work.tile([R, A_ROWS, P], BF16, tag="work")
         for x in range(A_ROWS):
             nc.tensor.transpose(
@@ -146,25 +139,39 @@ def tile_ffnwithscales_pb_s_kernel(
             in_=a_turned[:].rearrange("r x p -> r p x"),
         )
 
-        quantise_mlp(0)
-
         multipliers = sbuf.tile([P, D_TILES, F], F32)
         tiles_per_bank = 512 // F
-        for first_tile in range(0, D_TILES, tiles_per_bank):
-            product = work.tile([P, tiles_per_bank, F], F32, tag="work")
-            for i in range(tiles_per_bank):
-                rows = slice((first_tile + i) * P, (first_tile + i + 1) * P)
-                nc.tensor.matmul(
-                    out=product[:, i, :], lhsT=a_t[:, rows], rhs=b_sb[:], start=True, stop=True
+        products = []
+
+        def multiplier_tile(t):
+            i = t % tiles_per_bank
+            if i == 0:
+                products.append(work.tile([P, tiles_per_bank, F], F32, tag="work", name="product%d" % t))
+            nc.tensor.matmul(
+                out=products[-1][:, i, :], lhsT=a_t[:, t * P : (t + 1) * P], rhs=b_sb[:],
+                start=True, stop=True,
+            )
+            if i == tiles_per_bank - 1:
+                nc.vector.tensor_copy(
+                    out=multipliers[:, t - i : t + 1, :], in_=products[-1][:]
                 )
-            nc.vector.tensor_copy(
-                out=multipliers[:, first_tile : first_tile + tiles_per_bank, :], in_=product[:]
+
+        def quantise_g(c, h):
+            quantise_unit(
+                nc, sbuf, work, identity_f32, g_raw[c][h],
+                g_codes[c][h][:].bitcast(E5M2_X4), g_scales[c][h][:], "g%d_%d" % (c, h),
             )
 
-        quantise_grad_out(0)
-        for c in range(1, PASSES):
-            quantise_mlp(c)
-            quantise_grad_out(c)
+        quantise_mlp(0)
+        quantise_g(0, 0)
+        multiplier_tile(0)
+        quantise_g(0, 1)
+        multiplier_tile(1)
+        quantise_mlp(1)
+        multiplier_tile(2)
+        quantise_g(1, 0)
+        multiplier_tile(3)
+        quantise_g(1, 1)
 
         d_eff = [sums.tile([P, N_MOVING], F32, name="d_eff%d" % t) for t in range(D_TILES)]
         out_tiles = out.rearrange("(t q) f -> t q f", q=P)

@@ -15,11 +15,14 @@ PACK = 4
 BATCH, D, F, R, WIDTH = 4, 512, 256, 128, 256
 PAIR = 2
 PASSES = BATCH // PAIR
-ROWS = 2
-UNIT = ROWS * P
+HALF = P // PAIR
+ROWS = 4
+UNIT = ROWS * HALF
 G_UNITS = D // UNIT
 D_TILES = D // P
 TILES_PER_UNIT = UNIT // P
+ROWS_PER_TILE = ROWS // TILES_PER_UNIT
+OUT_STEP = D // HALF
 A_ROWS = D // P
 N_MOVING = 512
 WARM_MATMULS = 4
@@ -30,25 +33,29 @@ BYTES = 2 * (BATCH * F * WIDTH + BATCH * D * WIDTH + D * R + R * F) + 4 * D * F
 
 
 def load_unit(nc, sbuf, channels, name):
-    raw = sbuf.tile([P, PAIR * ROWS * WIDTH], BF16, name=name)
-    nc.sync.dma_start(out=raw[:].rearrange("p (u x) -> p u x", u=PAIR), in_=channels)
+    raw = sbuf.tile([P, ROWS * WIDTH], BF16, name=name)
+    nc.sync.dma_start(out=raw[:], in_=channels)
     return raw
 
 
-def quantise_unit(nc, sbuf, work, identity, raw, codes, scales, name):
+def quantise_unit(nc, sbuf, work, identity, raw, natural_order, codes, scales, name):
     words = raw[:].bitcast(F32)
-    turned = work.tile([P, PAIR, ROWS, P], F32, tag="work", name="turned_" + name)
-    for u in range(PAIR):
-        for r in range(ROWS):
-            first = (u * ROWS + r) * P
-            nc.tensor.transpose(
-                out=turned[:, u, r, :], in_=words[:, first : first + P], identity=identity[:]
-            )
+    turned = work.tile([P, ROWS, P], F32, tag="work", name="turned_" + name)
+    for r in range(ROWS):
+        nc.tensor.transpose(
+            out=turned[:, r, :], in_=words[:, r * P : (r + 1) * P], identity=identity[:]
+        )
     grouped = sbuf.tile([P, UNIT * PACK], BF16, name="grouped_" + name, align_bytes=64)
-    nc.scalar.copy(
-        out=grouped[:].bitcast(F32).rearrange("j (p r u) -> j p r u", r=ROWS, u=PAIR),
-        in_=turned[:].rearrange("j u r p -> j p r u"),
-    )
+    if natural_order:
+        nc.scalar.copy(
+            out=grouped[:].bitcast(F32).rearrange("j (q r u) -> j q r u", r=ROWS, u=PAIR),
+            in_=turned[:].rearrange("j r (u q) -> j q r u", u=PAIR),
+        )
+    else:
+        nc.scalar.copy(
+            out=grouped[:].bitcast(F32).rearrange("j (r q u) -> j r q u", r=ROWS, u=PAIR),
+            in_=turned[:].rearrange("j r (u q) -> j r q u", u=PAIR),
+        )
     nc.vector.quantize_mx(out=codes, scales=scales, in_=grouped[:])
 
 
@@ -87,24 +94,22 @@ def tile_ffnwithscales_pb_s_kernel(
             nc.vector.memset(m_codes[c][:, F:N_MOVING].bitcast(I32), 0)
             nc.vector.memset(m_scales[c][:, F:N_MOVING].bitcast(I32), 0)
 
-        m_view = mlp.rearrange("b (p r) one w -> p b (r one w)", r=ROWS)
-        g_view = grad_out.rearrange("b (h p r) one w -> h p b (r one w)", p=P, r=ROWS)
+        m_view = mlp.rearrange("(c u) (q r) one w -> c (u q) (r one w)", u=PAIR, r=ROWS)
+        g_view = grad_out.rearrange(
+            "(c u) (q h r) one w -> c h (u q) (r one w)", u=PAIR, h=G_UNITS, r=ROWS
+        )
         a_raw = sbuf.tile([P, A_ROWS * R], BF16)
         nc.sync.dma_start(
-            out=a_raw[:], in_=down_scale_A.rearrange("(p x) r -> p (x r)", x=A_ROWS)
+            out=a_raw[:], in_=down_scale_A.rearrange("(p x) k -> p (x k)", x=A_ROWS)
         )
         b_sb = sbuf.tile([R, F], BF16)
         nc.sync.dma_start(out=b_sb[:], in_=down_scale_B)
         m_raw = []
         g_raw = []
         for c in range(PASSES):
-            entries = slice(c * PAIR, (c + 1) * PAIR)
-            m_raw.append(load_unit(nc, sbuf, m_view[:, entries, :], "m_raw%d" % c))
+            m_raw.append(load_unit(nc, sbuf, m_view[c], "m_raw%d" % c))
             g_raw.append(
-                [
-                    load_unit(nc, sbuf, g_view[h, :, entries, :], "g_raw%d_%d" % (c, h))
-                    for h in range(G_UNITS)
-                ]
+                [load_unit(nc, sbuf, g_view[c, h], "g_raw%d_%d" % (c, h)) for h in range(G_UNITS)]
             )
 
         g_codes = [
@@ -124,8 +129,14 @@ def tile_ffnwithscales_pb_s_kernel(
 
         def quantise_mlp(c):
             quantise_unit(
-                nc, sbuf, work, identity_f32, m_raw[c],
+                nc, sbuf, work, identity_f32, m_raw[c], True,
                 m_codes[c][:, 0:F].bitcast(E4M3_X4), m_scales[c][:, 0:F], "m%d" % c,
+            )
+
+        def quantise_grad_out(c, h):
+            quantise_unit(
+                nc, sbuf, work, identity_f32, g_raw[c][h], False,
+                g_codes[c][h][:].bitcast(E5M2_X4), g_scales[c][h][:], "g%d_%d" % (c, h),
             )
 
         a_turned = work.tile([R, A_ROWS, P], BF16, tag="work")
@@ -135,8 +146,8 @@ def tile_ffnwithscales_pb_s_kernel(
             )
         a_t = sbuf.tile([R, D], BF16)
         nc.scalar.copy(
-            out=a_t[:].rearrange("r (p x) -> r p x", x=A_ROWS),
-            in_=a_turned[:].rearrange("r x p -> r p x"),
+            out=a_t[:].rearrange("k (h x q) -> k h x q", h=G_UNITS, x=A_ROWS),
+            in_=a_turned[:].rearrange("k x (q h) -> k h x q", h=G_UNITS),
         )
 
         multipliers = sbuf.tile([P, D_TILES, F], F32)
@@ -146,39 +157,33 @@ def tile_ffnwithscales_pb_s_kernel(
         def multiplier_tile(t):
             i = t % tiles_per_bank
             if i == 0:
-                products.append(work.tile([P, tiles_per_bank, F], F32, tag="work", name="product%d" % t))
+                products.append(
+                    work.tile([P, tiles_per_bank, F], F32, tag="work", name="product%d" % t)
+                )
             nc.tensor.matmul(
                 out=products[-1][:, i, :], lhsT=a_t[:, t * P : (t + 1) * P], rhs=b_sb[:],
                 start=True, stop=True,
             )
             if i == tiles_per_bank - 1:
-                nc.vector.tensor_copy(
-                    out=multipliers[:, t - i : t + 1, :], in_=products[-1][:]
-                )
-
-        def quantise_g(c, h):
-            quantise_unit(
-                nc, sbuf, work, identity_f32, g_raw[c][h],
-                g_codes[c][h][:].bitcast(E5M2_X4), g_scales[c][h][:], "g%d_%d" % (c, h),
-            )
+                nc.vector.tensor_copy(out=multipliers[:, t - i : t + 1, :], in_=products[-1][:])
 
         quantise_mlp(0)
-        quantise_g(0, 0)
+        quantise_grad_out(0, 0)
         multiplier_tile(0)
-        quantise_g(0, 1)
+        quantise_grad_out(0, 1)
         multiplier_tile(1)
         quantise_mlp(1)
         multiplier_tile(2)
-        quantise_g(1, 0)
+        quantise_grad_out(1, 0)
         multiplier_tile(3)
-        quantise_g(1, 1)
+        quantise_grad_out(1, 1)
 
         d_eff = [sums.tile([P, N_MOVING], F32, name="d_eff%d" % t) for t in range(D_TILES)]
-        out_tiles = out.rearrange("(t q) f -> t q f", q=P)
+        out_rows = out.rearrange("(q x) f -> x q f", x=OUT_STEP)
         for c in range(PASSES):
             for t in range(D_TILES):
-                h, i = divmod(t, TILES_PER_UNIT)
-                cols = slice(i * P, (i + 1) * P)
+                h, s = divmod(t, TILES_PER_UNIT)
+                cols = slice(s * P, (s + 1) * P)
                 nc.tensor.matmul_mx(
                     out=d_eff[t][:],
                     lhsT=g_codes[c][h][:, cols].bitcast(E5M2_X4),
@@ -191,4 +196,7 @@ def tile_ffnwithscales_pb_s_kernel(
         for t in range(D_TILES):
             result = sbuf.tile([P, F], F32, name="result%d" % t)
             nc.vector.tensor_mul(out=result[:], in0=d_eff[t][:, 0:F], in1=multipliers[:, t, :])
-            nc.sync.dma_start(out=out_tiles[t], in_=result[:])
+            for v in range(ROWS_PER_TILE):
+                nc.sync.dma_start(
+                    out=out_rows[t * ROWS_PER_TILE + v], in_=result[v * HALF : (v + 1) * HALF, :]
+                )

@@ -26,7 +26,8 @@ OUT_STEP = D // HALF
 A_ROWS = D // P
 N_MOVING = 512
 WARM_MATMULS = 4
-WORK_BANKS = 4
+M_BANK = ("bank0", "bank3")
+G_BANK = (("bank1", "bank2"), ("bank4", "bank5"))
 
 FLOPS = 2 * D * F * BATCH * WIDTH + 2 * D * F * R
 BYTES = 2 * (BATCH * F * WIDTH + BATCH * D * WIDTH + D * R + R * F) + 4 * D * F
@@ -38,9 +39,9 @@ def load_unit(nc, sbuf, channels, name):
     return raw
 
 
-def quantise_unit(nc, sbuf, work, identity, raw, natural_order, codes, scales, name):
+def quantise_unit(nc, sbuf, psum, bank, identity, raw, natural_order, codes, scales, name):
     words = raw[:].bitcast(F32)
-    turned = work.tile([P, ROWS, P], F32, tag="work", name="turned_" + name)
+    turned = psum.tile([P, ROWS, P], F32, tag=bank, name="turned_" + name)
     for r in range(ROWS):
         nc.tensor.transpose(
             out=turned[:, r, :], in_=words[:, r * P : (r + 1) * P], identity=identity[:]
@@ -65,13 +66,12 @@ def tile_ffnwithscales_pb_s_kernel(
     nc = tc.nc
     with (
         tc.tile_pool(name="sbuf", bufs=1) as sbuf,
-        tc.psum_pool(name="work", bufs=WORK_BANKS) as work,
-        tc.psum_pool(name="sums", bufs=1) as sums,
+        tc.psum_pool(name="psum", bufs=1) as psum,
         tc.manual_schedule(),
     ):
         warm = sbuf.tile([P, P], F32)
         nc.gpsimd.memset(warm[:], 0.0)
-        warm_out = work.tile([P, WARM_MATMULS, P], F32, tag="work")
+        warm_out = psum.tile([P, WARM_MATMULS, P], F32, tag="bank4")
         for i in range(WARM_MATMULS):
             nc.tensor.matmul(
                 out=warm_out[:, i, :], lhsT=warm[:], rhs=warm[:], start=True, stop=True
@@ -129,17 +129,17 @@ def tile_ffnwithscales_pb_s_kernel(
 
         def quantise_mlp(c):
             quantise_unit(
-                nc, sbuf, work, identity_f32, m_raw[c], True,
+                nc, sbuf, psum, M_BANK[c], identity_f32, m_raw[c], True,
                 m_codes[c][:, 0:F].bitcast(E4M3_X4), m_scales[c][:, 0:F], "m%d" % c,
             )
 
         def quantise_grad_out(c, h):
             quantise_unit(
-                nc, sbuf, work, identity_f32, g_raw[c][h], False,
+                nc, sbuf, psum, G_BANK[c][h], identity_f32, g_raw[c][h], False,
                 g_codes[c][h][:].bitcast(E5M2_X4), g_scales[c][h][:], "g%d_%d" % (c, h),
             )
 
-        a_turned = work.tile([R, A_ROWS, P], BF16, tag="work")
+        a_turned = psum.tile([R, A_ROWS, P], BF16, tag="bank5")
         for x in range(A_ROWS):
             nc.tensor.transpose(
                 out=a_turned[:, x, :], in_=a_raw[:, x * R : (x + 1) * R], identity=identity_bf16[:]
@@ -158,7 +158,10 @@ def tile_ffnwithscales_pb_s_kernel(
             i = t % tiles_per_bank
             if i == 0:
                 products.append(
-                    work.tile([P, tiles_per_bank, F], F32, tag="work", name="product%d" % t)
+                    psum.tile(
+                        [P, tiles_per_bank, F], F32, tag="bank%d" % (6 + t // tiles_per_bank),
+                        name="product%d" % t,
+                    )
                 )
             nc.tensor.matmul(
                 out=products[-1][:, i, :], lhsT=a_t[:, t * P : (t + 1) * P], rhs=b_sb[:],
@@ -178,7 +181,10 @@ def tile_ffnwithscales_pb_s_kernel(
         multiplier_tile(3)
         quantise_grad_out(1, 1)
 
-        d_eff = [sums.tile([P, N_MOVING], F32, name="d_eff%d" % t) for t in range(D_TILES)]
+        d_eff = [
+            psum.tile([P, N_MOVING], F32, tag="bank%d" % t, name="d_eff%d" % t)
+            for t in range(D_TILES)
+        ]
         out_rows = out.rearrange("(q x) f -> x q f", x=OUT_STEP)
         for c in range(PASSES):
             for t in range(D_TILES):

@@ -103,11 +103,12 @@ def tile_ffnwithscales_pb_s_kernel(
             out=a_raw[:], in_=down_scale_A.rearrange("(p x) k -> p (x k)", x=A_ROWS)
         )
         b_sb = sbuf.tile([R, F], BF16)
-        nc.sync.dma_start(out=b_sb[:], in_=down_scale_B)
         m_raw = []
         g_raw = []
         for c in range(PASSES):
             m_raw.append(load_unit(nc, sbuf, m_view[c], "m_raw%d" % c))
+            if c == 0:
+                nc.sync.dma_start(out=b_sb[:], in_=down_scale_B)
             g_raw.append(
                 [load_unit(nc, sbuf, g_view[c, h], "g_raw%d_%d" % (c, h)) for h in range(G_UNITS)]
             )
@@ -167,7 +168,7 @@ def tile_ffnwithscales_pb_s_kernel(
                 out=products[-1][:, i, :], lhsT=a_t[:, t * P : (t + 1) * P], rhs=b_sb[:],
                 start=True, stop=True,
             )
-            if i == tiles_per_bank - 1:
+            if t == tiles_per_bank - 1:
                 nc.vector.tensor_copy(out=multipliers[:, t - i : t + 1, :], in_=products[-1][:])
 
         quantise_mlp(0)
@@ -180,6 +181,7 @@ def tile_ffnwithscales_pb_s_kernel(
         quantise_grad_out(1, 0)
         multiplier_tile(3)
         quantise_grad_out(1, 1)
+        nc.scalar.copy(out=multipliers[:, tiles_per_bank:D_TILES, :], in_=products[-1][:])
 
         d_eff = [
             psum.tile([P, N_MOVING], F32, tag="bank%d" % t, name="d_eff%d" % t)

@@ -46,7 +46,7 @@ def quantise_unit(nc, sbuf, psum, bank, identity, raw, natural_order, codes, sca
         nc.tensor.transpose(
             out=turned[:, r, :], in_=words[:, r * P : (r + 1) * P], identity=identity[:]
         )
-    grouped = sbuf.tile([P, UNIT * PACK], BF16, name="grouped_" + name, align_bytes=64)
+    grouped = sbuf.tile([P, UNIT * PACK], BF16, name="grouped_" + name, align_bytes=256)
     if natural_order:
         nc.scalar.copy(
             out=grouped[:].bitcast(F32).rearrange("j (q r u) -> j q r u", r=ROWS, u=PAIR),
@@ -83,11 +83,11 @@ def tile_ffnwithscales_pb_s_kernel(
         make_identity(nc, identity_f32[:])
 
         m_codes = [
-            sbuf.tile([P, N_MOVING], U32, name="m_codes%d" % c, align_bytes=64)
+            sbuf.tile([P, N_MOVING], U32, name="m_codes%d" % c, align_bytes=256)
             for c in range(PASSES)
         ]
         m_scales = [
-            sbuf.tile([P, N_MOVING], U8, name="m_scales%d" % c, align_bytes=64)
+            sbuf.tile([P, N_MOVING], U8, name="m_scales%d" % c, align_bytes=256)
             for c in range(PASSES)
         ]
         for c in range(PASSES):
@@ -115,14 +115,14 @@ def tile_ffnwithscales_pb_s_kernel(
 
         g_codes = [
             [
-                sbuf.tile([P, UNIT], U32, name="g_codes%d_%d" % (c, h), align_bytes=64)
+                sbuf.tile([P, UNIT], U32, name="g_codes%d_%d" % (c, h), align_bytes=256)
                 for h in range(G_UNITS)
             ]
             for c in range(PASSES)
         ]
         g_scales = [
             [
-                sbuf.tile([P, UNIT], U8, name="g_scales%d_%d" % (c, h), align_bytes=64)
+                sbuf.tile([P, UNIT], U8, name="g_scales%d_%d" % (c, h), align_bytes=256)
                 for h in range(G_UNITS)
             ]
             for c in range(PASSES)

import concourse.mybir as mybir
from concourse.masks import make_identity

BF16 = mybir.dt.bfloat16
F32 = mybir.dt.float32
I32 = mybir.dt.int32
U32 = mybir.dt.uint32
U8 = mybir.dt.uint8
E4M3_X4 = mybir.dt.float8_e4m3fn_x4
E5M2_X4 = mybir.dt.float8_e5m2_x4

P = 128
PACK = 4

BATCH, D, F, R, WIDTH = 4, 512, 256, 128, 256
PAIR = 2
PASSES = BATCH // PAIR
HALF = P // PAIR
ROWS = 4
UNIT = ROWS * HALF
G_UNITS = D // UNIT
D_TILES = D // P
TILES_PER_UNIT = UNIT // P
ROWS_PER_TILE = ROWS // TILES_PER_UNIT
OUT_STEP = D // HALF
A_ROWS = D // P
N_MOVING = 512
WARM_MATMULS = 4
M_BANK = ("bank0", "bank3")
G_BANK = (("bank1", "bank2"), ("bank4", "bank5"))

FLOPS = 2 * D * F * BATCH * WIDTH + 2 * D * F * R
BYTES = 2 * (BATCH * F * WIDTH + BATCH * D * WIDTH + D * R + R * F) + 4 * D * F


def load_unit(nc, sbuf, channels, name):
    raw = sbuf.tile([P, ROWS * WIDTH], BF16, name=name)
    nc.sync.dma_start(out=raw[:], in_=channels)
    return raw


def quantise_unit(nc, sbuf, psum, bank, identity, raw, natural_order, codes, scales, name):
    words = raw[:].bitcast(F32)
    turned = psum.tile([P, ROWS, P], F32, tag=bank, name="turned_" + name)
    for r in range(ROWS):
        nc.tensor.transpose(
            out=turned[:, r, :], in_=words[:, r * P : (r + 1) * P], identity=identity[:]
        )
    grouped = sbuf.tile([P, UNIT * PACK], BF16, name="grouped_" + name, align_bytes=256)
    if natural_order:
        nc.scalar.copy(
            out=grouped[:].bitcast(F32).rearrange("j (q r u) -> j q r u", r=ROWS, u=PAIR),
            in_=turned[:].rearrange("j r (u q) -> j q r u", u=PAIR),
        )
    else:
        nc.scalar.copy(
            out=grouped[:].bitcast(F32).rearrange("j (r q u) -> j r q u", r=ROWS, u=PAIR),
            in_=turned[:].rearrange("j r (u q) -> j r q u", u=PAIR),
        )
    nc.vector.quantize_mx(out=codes, scales=scales, in_=grouped[:])


def tile_ffnwithscales_pb_s_kernel(
    tc, mlp, down_snapped, down_scale_A, down_scale_B, grad_out, out
):
    nc = tc.nc
    with (
        tc.tile_pool(name="sbuf", bufs=1) as sbuf,
        tc.psum_pool(name="psum", bufs=1) as psum,
        tc.manual_schedule(),
    ):
        warm = sbuf.tile([P, P], F32)
        nc.gpsimd.memset(warm[:], 0.0)
        warm_out = psum.tile([P, WARM_MATMULS, P], F32, tag="bank4")
        for i in range(WARM_MATMULS):
            nc.tensor.matmul(
                out=warm_out[:, i, :], lhsT=warm[:], rhs=warm[:], start=True, stop=True
            )

        identity_bf16 = sbuf.tile([P, P], BF16)
        make_identity(nc, identity_bf16[:])
        identity_f32 = sbuf.tile([P, P], F32)
        make_identity(nc, identity_f32[:])

        m_codes = [
            sbuf.tile([P, N_MOVING], U32, name="m_codes%d" % c, align_bytes=256)
            for c in range(PASSES)
        ]
        m_scales = [
            sbuf.tile([P, N_MOVING], U8, name="m_scales%d" % c, align_bytes=256)
            for c in range(PASSES)
        ]
        for c in range(PASSES):
            nc.vector.memset(m_codes[c][:, F:N_MOVING].bitcast(I32), 0)
            nc.vector.memset(m_scales[c][:, F:N_MOVING].bitcast(I32), 0)

        m_view = mlp.rearrange("(c u) (q r) one w -> c (u q) (r one w)", u=PAIR, r=ROWS)
        g_view = grad_out.rearrange(
            "(c u) (q h r) one w -> c h (u q) (r one w)", u=PAIR, h=G_UNITS, r=ROWS
        )
        a_raw = sbuf.tile([P, A_ROWS * R], BF16)
        nc.sync.dma_start(
            out=a_raw[:], in_=down_scale_A.rearrange("(p x) k -> p (x k)", x=A_ROWS)
        )
        b_sb = sbuf.tile([R, F], BF16)
        m_raw = []
        g_raw = []
        for c in range(PASSES):
            m_raw.append(load_unit(nc, sbuf, m_view[c], "m_raw%d" % c))
            if c == 0:
                nc.sync.dma_start(out=b_sb[:], in_=down_scale_B)
            g_raw.append(
                [load_unit(nc, sbuf, g_view[c, h], "g_raw%d_%d" % (c, h)) for h in range(G_UNITS)]
            )

        g_codes = [
            [
                sbuf.tile([P, UNIT], U32, name="g_codes%d_%d" % (c, h), align_bytes=256)
                for h in range(G_UNITS)
            ]
            for c in range(PASSES)
        ]
        g_scales = [
            [
                sbuf.tile([P, UNIT], U8, name="g_scales%d_%d" % (c, h), align_bytes=256)
                for h in range(G_UNITS)
            ]
            for c in range(PASSES)
        ]

        def quantise_mlp(c):
            quantise_unit(
                nc, sbuf, psum, M_BANK[c], identity_f32, m_raw[c], True,
                m_codes[c][:, 0:F].bitcast(E4M3_X4), m_scales[c][:, 0:F], "m%d" % c,
            )

        def quantise_grad_out(c, h):
            quantise_unit(
                nc, sbuf, psum, G_BANK[c][h], identity_f32, g_raw[c][h], False,
                g_codes[c][h][:].bitcast(E5M2_X4), g_scales[c][h][:], "g%d_%d" % (c, h),
            )

        a_turned = psum.tile([R, A_ROWS, P], BF16, tag="bank5")
        for x in range(A_ROWS):
            nc.tensor.transpose(
                out=a_turned[:, x, :], in_=a_raw[:, x * R : (x + 1) * R], identity=identity_bf16[:]
            )
        a_t = sbuf.tile([R, D], BF16)
        nc.scalar.copy(
            out=a_t[:].rearrange("k (h x q) -> k h x q", h=G_UNITS, x=A_ROWS),
            in_=a_turned[:].rearrange("k x (q h) -> k h x q", h=G_UNITS),
        )

        multipliers = sbuf.tile([P, D_TILES, F], F32)
        tiles_per_bank = 512 // F
        products = []

        def multiplier_tile(t):
            i = t % tiles_per_bank
            if i == 0:
                products.append(
                    psum.tile(
                        [P, tiles_per_bank, F], F32, tag="bank%d" % (6 + t // tiles_per_bank),
                        name="product%d" % t,
                    )
                )
            nc.tensor.matmul(
                out=products[-1][:, i, :], lhsT=a_t[:, t * P : (t + 1) * P], rhs=b_sb[:],
                start=True, stop=True,
            )
            if t == tiles_per_bank - 1:
                nc.vector.tensor_copy(out=multipliers[:, t - i : t + 1, :], in_=products[-1][:])

        quantise_mlp(0)
        quantise_grad_out(0, 0)
        multiplier_tile(0)
        quantise_grad_out(0, 1)
        multiplier_tile(1)
        quantise_mlp(1)
        multiplier_tile(2)
        quantise_grad_out(1, 0)
        multiplier_tile(3)
        quantise_grad_out(1, 1)
        nc.scalar.copy(out=multipliers[:, tiles_per_bank:D_TILES, :], in_=products[-1][:])

        d_eff = [
            psum.tile([P, N_MOVING], F32, tag="bank%d" % t, name="d_eff%d" % t)
            for t in range(D_TILES)
        ]
        out_rows = out.rearrange("(q x) f -> x q f", x=OUT_STEP)
        for c in range(PASSES):
            for t in range(D_TILES):
                h, s = divmod(t, TILES_PER_UNIT)
                cols = slice(s * P, (s + 1) * P)
                nc.tensor.matmul_mx(
                    out=d_eff[t][:],
                    lhsT=g_codes[c][h][:, cols].bitcast(E5M2_X4),
                    lhsT_scale=g_scales[c][h][:, cols],
                    rhs=m_codes[c][:].bitcast(E4M3_X4),
                    rhs_scale=m_scales[c][:],
                    start=(c == 0),
                    stop=(c == PASSES - 1),
                )
        for t in range(D_TILES):
            result = sbuf.tile([P, F], F32, name="result%d" % t)
            nc.vector.tensor_mul(out=result[:], in0=d_eff[t][:, 0:F], in1=multipliers[:, t, :])
            for v in range(ROWS_PER_TILE):
                nc.sync.dma_start(
                    out=out_rows[t * ROWS_PER_TILE + v], in_=result[v * HALF : (v + 1) * HALF, :]
                )
